import numpy as np
import ml_dtypes


def mxq(x, axis, fmt="e4m3"):
    dtype, down = {"e4m3": (ml_dtypes.float8_e4m3fn, 7), "e5m2": (ml_dtypes.float8_e5m2, 14)}[fmt]
    v = np.moveaxis(np.asarray(x, np.float32).astype(ml_dtypes.bfloat16).astype(np.float64), axis, -1)
    blocks = v.reshape(v.shape[:-1] + (-1, 32))
    amax = np.abs(blocks).max(-1, keepdims=True)
    byte = np.maximum(np.where(amax > 0, np.frexp(amax)[1] - 1 + 127, 0) - down, 1)
    scale = np.exp2(byte - 127.0)
    codes = (blocks / scale).astype(np.float32).astype(dtype).astype(np.float64)
    return np.moveaxis((codes * scale).reshape(v.shape), -1, axis)


WIDE = False


def mx_kscale(k):
    if not WIDE:
        return np.ones(k)
    levels = np.array([10, -10, 5, -5, 0])
    if k % 512:
        return np.exp2(np.random.permutation(np.resize(levels, k // 32))).repeat(32)
    a = np.empty((k // 512, 16))
    for p in range(k // 512):
        a[p, :8] = np.random.permutation(np.resize(levels, 8))
        for g in range(8):
            far = levels[np.abs(levels - a[p, g]) >= 10]
            a[p, g + 8] = far[np.random.randint(len(far))]
    return np.exp2(a.ravel()).repeat(32)


BF16 = ml_dtypes.bfloat16


def bf(x):
    return np.asarray(x, np.float32).astype(BF16)


def f64(x):
    return np.asarray(x).astype(np.float64)


E, T, H, D, R = 4, 256, 1024, 1024, 128
SCALE = 2.0


def draw0():
    s = mx_kscale(D)
    return {"h": bf(np.random.standard_normal((E, T, D)) * 0.8 * s),
            "low_d": bf(np.random.standard_normal((E, T, R)) * 1.2),
            "W_d": bf(np.random.standard_normal((E, H, D)) * 1.5 / np.sqrt(D) / s),
            "B_d": bf(np.random.standard_normal((E, H, R)) * 0.3 / np.sqrt(R))}


def core(h, low_d, W_d, B_d):
    base = mxq(f64(h), 2, "e4m3") @ mxq(f64(W_d), 2, "e4m3").transpose(0, 2, 1)
    delta = f64(low_d) @ f64(B_d).transpose(0, 2, 1)
    out = base + SCALE * delta
    return out.reshape(-1, H)


def e4m3fn_bytes(y):
    return np.clip(np.asarray(y, np.float64), -448.0, 448.0).astype(np.float32).astype(ml_dtypes.float8_e4m3fn).view(np.uint8)


def e4m3fn_values(b):
    return np.asarray(b, np.uint8).view(ml_dtypes.float8_e4m3fn).astype(np.float64)


def setup_inputs():
    d = draw0()
    x0 = np.asarray(d['W_d']).astype(np.float64)
    s = (np.max(np.abs(x0), axis=(0, 1), keepdims=True) / 448.0).astype(np.float32)
    out = {}
    for k, v in d.items():
        if k == 'W_d':
            out['W_d_bytes'] = e4m3fn_bytes(x0 / s.astype(np.float64))
            out['W_d_scale'] = s
        else:
            out[k] = v
    return out


def reference(h, low_d, W_d_bytes, W_d_scale, B_d):
    return core(h, low_d, e4m3fn_values(W_d_bytes) * W_d_scale.astype(np.float64), B_d)

@@ -1,0 +1,317 @@
+from contextlib import ExitStack
+
+import concourse.mybir as mybir
+from concourse.masks import make_identity
+
+E, T, H, D, R = 4, 256, 1024, 1024, 128
+LORA_SCALE = 2.0
+FLOPS = 2 * E * T * H * (D + R)
+
+F32 = mybir.dt.float32
+BF16 = mybir.dt.bfloat16
+U32 = mybir.dt.uint32
+U8 = mybir.dt.uint8
+FP8 = mybir.dt.float8_e4m3fn
+FP8X4 = mybir.dt.float8_e4m3fn_x4
+MULT = mybir.AluOpType.mult
+ADD = mybir.AluOpType.add
+COPY = mybir.ActivationFunctionType.Copy
+
+P = 128
+PASSES = D // 512
+UNIT_N = 512
+UNIT_ROWTILES = UNIT_N // P
+UNITS = E * H // UNIT_N
+M_TILES = T // P
+
+
+def tile_loralinearexpertswrapper_pb_kernel(tc, h, low_d, W_d_bytes, W_d_scale, B_d, out):
+    nc = tc.nc
+    with ExitStack() as ctx:
+        keep = ctx.enter_context(tc.tile_pool(name="keep", bufs=1))
+        work = ctx.enter_context(tc.tile_pool(name="work", bufs=3))
+        ps_t = ctx.enter_context(tc.psum_pool(name="ps_t", bufs=4))
+        ps_b = ctx.enter_context(tc.psum_pool(name="ps_b", bufs=2))
+        ps_f = ctx.enter_context(tc.psum_pool(name="ps_f", bufs=2))
+        ctx.enter_context(tc.manual_schedule())
+
+        scale2 = keep.tile([P, 2, D], F32, name="scale2")
+        nc.scalar.dma_start(out=scale2[:, 0, :], in_=W_d_scale.rearrange("a b k -> (a b k)").partition_broadcast(P))
+
+        warm_in = keep.tile([P, 1], F32, name="warm_in")
+        warm_out = keep.tile([P, 1], F32, name="warm_out")
+        nc.vector.memset(warm_in[:], 0.0)
+        nc.scalar.activation(out=warm_out[:], in_=warm_in[:], func=COPY)
+
+        ident_f = keep.tile([P, P], F32, name="ident_f")
+        make_identity(nc, ident_f[:])
+        ident_b = keep.tile([P, P], BF16, name="ident_b")
+        make_identity(nc, ident_b[:])
+
+        w_rows = W_d_bytes.rearrange("e (c p) k -> e c p k", p=P)
+        h_rows = h.rearrange("e (m p) k -> e p m k", p=P)
+        b_rows = B_d.rearrange("e (c p) r -> e p c r", p=P)
+
+        wbytes = {}
+
+        def load_w(u, j0, nj):
+            e, c0 = u // 2, (u % 2) * UNIT_ROWTILES + j0
+            t = keep.tile([P, nj, D], U8, name="wbytes_%d_%d" % (u, j0))
+            nc.sync.dma_start(out=t[:], in_=w_rows[e, c0:c0 + nj].rearrange("c p k -> p c k"))
+            for j in range(nj):
+                wbytes[(u, j0 + j, 1)] = t[:, j, :]
+            for j in range(0, nj - 1, 2):
+                wbytes[(u, j0 + j, 2)] = t[:, j:j + 2, :].rearrange("p c k -> p (c k)")
+
+        h_sb = {}
+
+        def load_h(e):
+            t = keep.tile([P, M_TILES, D], BF16, name="h_sb%d" % e)
+            nc.sync.dma_start(out=t[:], in_=h_rows[e])
+            h_sb[e] = t
+
+        b_sb = {}
+
+        def load_b(e):
+            t = keep.tile([P, H // P, R], BF16, name="b_sb%d" % e)
+            nc.sync.dma_start(out=t[:], in_=b_rows[e])
+            b_sb[e] = t
+
+        load_w(0, 0, 1)
+        load_h(0)
+        load_w(0, 1, 1)
+        load_w(0, 2, 2)
+        low_sb = keep.tile([P, E * M_TILES, R], BF16, name="low_sb")
+        nc.sync.dma_start(out=low_sb[:], in_=low_d.rearrange("e (m p) r -> p (e m) r", p=P))
+        load_b(0)
+        load_w(1, 0, 4)
+        for e in range(1, E):
+            load_w(2 * e, 0, 4)
+            load_h(e)
+            load_b(e)
+            load_w(2 * e + 1, 0, 4)
+
+        nc.scalar.copy(out=scale2[:, 1, :], in_=scale2[:, 0, :])
+
+        grouped = {}
+        hgrouped = {}
+        hq = {}
+        hs = {}
+        wq = {}
+        ws = {}
+        b_t = {}
+        delta2 = {}
+        acc = {}
+        base_t = {}
+        fin = {}
+
+        def new_grouped(u):
+            grouped[u] = work.tile([P, PASSES, UNIT_N, 4], BF16, name="grouped", tag="grouped", bufs=4, align_bytes=64)
+
+        def turn_words(src_bf16, dst_words):
+            words = src_bf16.bitcast(F32)
+            tp = ps_t.tile([P, PASSES, 2, P], F32, name="tp", tag="tp")
+            for g in range(PASSES):
+                for u in range(2):
+                    nc.tensor.transpose(tp[:, g, u, :], words[:, 256 * g + u:256 * (g + 1):2], ident_f[:])
+            nc.scalar.copy(out=dst_words, in_=tp[:].rearrange("p g u r -> p g r u"))
+
+        wbf = {}
+
+        def product(u, j0, nj):
+            t = work.tile([P, nj * D], BF16, name="wbf", tag="wbf", bufs=4, align_bytes=64)
+            nc.vector.tensor_tensor(out=t[:], in0=wbytes[(u, j0, nj)].bitcast(FP8),
+                                    in1=scale2[:, 0:nj, :].rearrange("p c k -> p (c k)"), op=MULT)
+            wbf[(u, j0)] = t
+
+        def turn_w(u, j0, nj):
+            if j0 == 0:
+                new_grouped(u)
+            for j in range(nj):
+                turn_words(wbf[(u, j0)][:, j * D:(j + 1) * D],
+                           grouped[u][:].bitcast(F32)[:, :, (j0 + j) * P:(j0 + j + 1) * P, :])
+
+        def turn_h(e, m):
+            if m == 0:
+                hgrouped[e] = work.tile([P, PASSES, T, 4], BF16, name="hgrouped", tag="hgrouped", bufs=2, align_bytes=64)
+            turn_words(h_sb[e][:, m, :], hgrouped[e][:].bitcast(F32)[:, :, m * P:(m + 1) * P, :])
+
+        def quant_h(e):
+            hq[e] = keep.tile([P, PASSES * T], U32, name="hq%d" % e, align_bytes=64)
+            hs[e] = keep.tile([P, PASSES * T], U8, name="hs%d" % e, align_bytes=64)
+            nc.vector.quantize_mx(out=hq[e][:].bitcast(FP8X4), scales=hs[e][:],
+                                  in_=hgrouped[e][:].rearrange("p g n t -> p (g n t)"))
+
+        low_t = keep.tile([P, E * T], BF16, name="low_t")
+
+        def turn_low():
+            tl = ps_t.tile([P, E * M_TILES, P], BF16, name="tl", tag="tp")
+            for i in range(E * M_TILES):
+                nc.tensor.transpose(tl[:, i, :], low_sb[:, i, :], ident_b[:])
+            nc.scalar.activation(out=low_t[:], in_=tl[:].rearrange("p i r -> p (i r)"), func=COPY, scale=LORA_SCALE)
+
+        def turn_b(e, half):
+            if half == 0:
+                b_t[e] = keep.tile([P, H], BF16, name="b_t%d" % e)
+            tb = ps_t.tile([P, 4, P], BF16, name="tb", tag="tp")
+            for c in range(4):
+                nc.tensor.transpose(tb[:, c, :], b_sb[e][:, 4 * half + c, :], ident_b[:])
+            nc.scalar.copy(out=b_t[e][:, 512 * half:512 * (half + 1)], in_=tb[:].rearrange("p c r -> p (c r)"))
+
+        def open_fin(u):
+            e, nh = u // 2, u % 2
+            for m in range(M_TILES):
+                f = ps_f.tile([P, UNIT_N], F32, name="fin", tag="fin")
+                nc.tensor.matmul(out=f[:], lhsT=low_t[:, (e * M_TILES + m) * P:(e * M_TILES + m + 1) * P],
+                                 rhs=b_t[e][:, nh * UNIT_N:(nh + 1) * UNIT_N], start=True, stop=False)
+                fin[(u, m)] = f
+
+        def quant_w(u):
+            wq[u] = work.tile([P, PASSES * UNIT_N], U32, name="wq", tag="wq", bufs=3, align_bytes=64)
+            ws[u] = work.tile([P, PASSES * UNIT_N], U8, name="ws", tag="ws", bufs=3, align_bytes=64)
+            nc.vector.quantize_mx(out=wq[u][:].bitcast(FP8X4), scales=ws[u][:],
+                                  in_=grouped[u][:].rearrange("p g n t -> p (g n t)"))
+
+        def base_turned(u):
+            e = u // 2
+            for half in range(2):
+                bt = ps_b.tile([P, 2, T], F32, name="bt", tag="bt")
+                for cc in range(2):
+                    c = half * 2 + cc
+                    for g in range(PASSES):
+                        wc = slice(g * UNIT_N + c * P, g * UNIT_N + (c + 1) * P)
+                        hc = slice(g * T, (g + 1) * T)
+                        nc.tensor.matmul_mx(out=bt[:, cc, :], lhsT=wq[u][:, wc].bitcast(FP8X4), lhsT_scale=ws[u][:, wc],
+                                            rhs=hq[e][:, hc].bitcast(FP8X4), rhs_scale=hs[e][:, hc],
+                                            start=(g == 0), stop=(g == PASSES - 1))
+                sb = work.tile([P, 2, T], F32, name="base_t", tag="base_t", bufs=4)
+                nc.scalar.copy(out=sb[:], in_=bt[:])
+                base_t[(u, half)] = sb
+
+        def add_base(u):
+            for m in range(M_TILES):
+                for c in range(4):
+                    nc.tensor.matmul(out=fin[(u, m)][:, c * P:(c + 1) * P],
+                                     lhsT=base_t[(u, c // 2)][:, c % 2, m * P:(m + 1) * P], rhs=ident_f[:],
+                                     is_transpose=True, start=False, stop=(c == 3))
+
+        def store(u, m, o):
+            e, nh = u // 2, u % 2
+            r0 = (e * M_TILES + m) * P
+            nc.sync.dma_start(out=out[r0:r0 + P, nh * UNIT_N:(nh + 1) * UNIT_N], in_=o[:])
+
+        def finish(u, m, on_vector):
+            o = work.tile([P, UNIT_N], F32, name="o_sb", tag="o_sb", bufs=4)
+            if on_vector:
+                nc.vector.tensor_copy(out=o[:], in_=fin[(u, m)][:])
+            else:
+                nc.scalar.copy(out=o[:], in_=fin[(u, m)][:])
+            store(u, m, o)
+
+        def lora_closed(u):
+            e, nh = u // 2, u % 2
+            for m in range(M_TILES):
+                dl = ps_t.tile([P, UNIT_N], F32, name="dl", tag="tp")
+                nc.tensor.matmul(out=dl[:], lhsT=low_t[:, (e * M_TILES + m) * P:(e * M_TILES + m + 1) * P],
+                                 rhs=b_t[e][:, nh * UNIT_N:(nh + 1) * UNIT_N], start=True, stop=True)
+                d2 = work.tile([P, UNIT_N], F32, name="d2", tag="d2", bufs=4)
+                nc.scalar.copy(out=d2[:], in_=dl[:])
+                delta2[(u, m)] = d2
+
+        def base(u, pool, tag):
+            e = u // 2
+            for m in range(M_TILES):
+                a = pool.tile([P, UNIT_N], F32, name="acc", tag=tag)
+                for g in range(PASSES):
+                    hc = slice(g * T + m * P, g * T + (m + 1) * P)
+                    wc = slice(g * UNIT_N, (g + 1) * UNIT_N)
+                    nc.tensor.matmul_mx(out=a[:], lhsT=hq[e][:, hc].bitcast(FP8X4), lhsT_scale=hs[e][:, hc],
+                                        rhs=wq[u][:, wc].bitcast(FP8X4), rhs_scale=ws[u][:, wc],
+                                        start=(g == 0), stop=(g == PASSES - 1))
+                acc[(u, m)] = a
+
+        def vadd(u):
+            for m in range(M_TILES):
+                o = work.tile([P, UNIT_N], F32, name="o_sb", tag="o_sb", bufs=4)
+                nc.vector.tensor_tensor(out=o[:], in0=acc[(u, m)][:], in1=delta2[(u, m)][:], op=ADD)
+                store(u, m, o)
+
+        PE_ADD_UNITS = UNITS - 2
+
+        zeros = keep.tile([P, 512], BF16, name="zeros")
+        nc.vector.memset(zeros[:], 0.0)
+
+        def plain_warm(n):
+            w = ps_b.tile([P, 512], F32, name="warm_p", tag="bt")
+            for i in range(n):
+                nc.tensor.matmul(out=w[:], lhsT=ident_b[:], rhs=zeros[:], start=True, stop=True)
+
+        def keep_warm(n):
+            w = ps_b.tile([P, 512], F32, name="warm_ps", tag="bt")
+            for i in range(n):
+                nc.tensor.matmul_mx(out=w[:], lhsT=hq[0][:, 0:P].bitcast(FP8X4), lhsT_scale=hs[0][:, 0:P],
+                                    rhs=hq[0][:, 0:512].bitcast(FP8X4), rhs_scale=hs[0][:, 0:512],
+                                    start=True, stop=True)
+
+        LAST = UNITS - 1
+        plain_warm(4)
+        turn_h(0, 0)
+        turn_h(0, 1)
+        product(0, 0, 1)
+        product(0, 1, 1)
+        plain_warm(2)
+        turn_w(0, 0, 1)
+        turn_w(0, 1, 1)
+        plain_warm(2)
+        turn_low()
+        product(0, 2, 2)
+        quant_h(0)
+        for s in range(UNITS):
+            c = s - 1
+            more = s < LAST
+            pe_add = 0 <= c < PE_ADD_UNITS
+            if more:
+                product(s + 1, 0, 2)
+            if pe_add:
+                base_turned(c)
+            elif c >= 0:
+                base(c, ps_b, "bt")
+            else:
+                keep_warm(4)
+            if more:
+                turn_w(s, 2, 2)
+            if s == 0:
+                turn_b(0, 0)
+                turn_b(0, 1)
+            elif s % 2 == 1 and s // 2 + 1 < E:
+                turn_b(s // 2 + 1, 0)
+            elif s % 2 == 0 and s // 2 < E and s >= 2:
+                turn_b(s // 2, 1)
+            if pe_add:
+                open_fin(c)
+                add_base(c)
+            elif more:
+                keep_warm(2)
+            if s % 2 == 0 and s // 2 + 1 < E:
+                turn_h(s // 2 + 1, 0)
+            elif s % 2 == 1 and s // 2 + 1 < E:
+                turn_h(s // 2 + 1, 1)
+            if pe_add:
+                finish(c, 0, False)
+                finish(c, 1, False)
+            if s == PE_ADD_UNITS:
+                lora_closed(PE_ADD_UNITS)
+                lora_closed(PE_ADD_UNITS + 1)
+            elif more:
+                keep_warm(2)
+            if more:
+                product(s + 1, 2, 2)
+                turn_w(s + 1, 0, 2)
+            if s + 1 == LAST:
+                turn_w(LAST, 2, 2)
+            if s % 2 == 0 and s >= 2:
+                quant_h(s // 2)
+            quant_w(s)
+        vadd(LAST - 1)
+        base(LAST, ps_f, "fin")
+        vadd(LAST)

@@ -299,16 +299,15 @@ def tile_loralinearexpertswrapper_pb_kernel(tc, h, low_d, W_d_bytes, W_d_scale, 
             if pe_add:
                 finish(c, 0, False)
                 finish(c, 1, False)
-            if s == PE_ADD_UNITS:
-                lora_closed(PE_ADD_UNITS)
-                lora_closed(PE_ADD_UNITS + 1)
-            elif more:
+            if more:
                 keep_warm(2)
             if more:
                 product(s + 1, 2, 2)
                 turn_w(s + 1, 0, 2)
             if s + 1 == LAST:
                 turn_w(LAST, 2, 2)
+                lora_closed(LAST - 1)
+                lora_closed(LAST)
             if s % 2 == 0 and s >= 2:
                 quant_h(s // 2)
             quant_w(s)

@@ -81,10 +81,10 @@ def tile_loralinearexpertswrapper_pb_kernel(tc, h, low_d, W_d_bytes, W_d_scale, 
         load_h(0)
         load_w(0, 1, 1)
         load_w(0, 2, 2)
+        load_w(1, 0, 4)
         low_sb = keep.tile([P, E * M_TILES, R], BF16, name="low_sb")
         nc.sync.dma_start(out=low_sb[:], in_=low_d.rearrange("e (m p) r -> p (e m) r", p=P))
         load_b(0)
-        load_w(1, 0, 4)
         for e in range(1, E):
             load_w(2 * e, 0, 4)
             load_h(e)

@@ -120,8 +120,8 @@ def tile_loralinearexpertswrapper_pb_kernel(tc, h, low_d, W_d_bytes, W_d_scale, 
 
         def product(u, j0, nj):
             t = work.tile([P, nj * D], BF16, name="wbf", tag="wbf", bufs=4, align_bytes=64)
-            nc.vector.tensor_tensor(out=t[:], in0=wbytes[(u, j0, nj)].bitcast(FP8),
-                                    in1=scale2[:, 0:nj, :].rearrange("p c k -> p (c k)"), op=MULT)
+            nc.vector.tensor_tensor(out=t[:], in0=scale2[:, 0:nj, :].rearrange("p c k -> p (c k)"),
+                                    in1=wbytes[(u, j0, nj)].bitcast(FP8), op=MULT)
             wbf[(u, j0)] = t
 
         def turn_w(u, j0, nj):

@@ -36,7 +36,8 @@ def tile_loralinearexpertswrapper_pb_kernel(tc, h, low_d, W_d_bytes, W_d_scale, 
         ctx.enter_context(tc.manual_schedule())
 
         scale2 = keep.tile([P, 2, D], F32, name="scale2")
-        nc.scalar.dma_start(out=scale2[:, 0, :], in_=W_d_scale.rearrange("a b k -> (a b k)").partition_broadcast(P))
+        scale_k = keep.tile([P, PASSES, 4], F32, name="scale_k")
+        nc.sync.dma_start(out=scale_k[:], in_=W_d_scale.rearrange("a b (g p t) -> p (a b g) t", p=P, t=4))
 
         warm_in = keep.tile([P, 1], F32, name="warm_in")
         warm_out = keep.tile([P, 1], F32, name="warm_out")
@@ -91,7 +92,17 @@ def tile_loralinearexpertswrapper_pb_kernel(tc, h, low_d, W_d_bytes, W_d_scale, 
             load_b(e)
             load_w(2 * e + 1, 0, 4)
 
-        nc.scalar.copy(out=scale2[:, 1, :], in_=scale2[:, 0, :])
+        def spread_scales():
+            for g in range(PASSES):
+                sp = ps_t.tile([P, 4, P], F32, name="sp", tag="tp")
+                for t in range(4):
+                    nc.tensor.transpose(sp[:, t, :], scale_k[:, g, t:t + 1].to_broadcast([P, P]), ident_f[:])
+                dst = scale2[:, 0, 512 * g:512 * (g + 1)].rearrange("p (n t) -> p n t", t=4)
+                if g == 0:
+                    nc.vector.tensor_copy(out=dst, in_=sp[:].rearrange("p t n -> p n t"))
+                else:
+                    nc.scalar.copy(out=dst, in_=sp[:].rearrange("p t n -> p n t"))
+            nc.scalar.copy(out=scale2[:, 1, :], in_=scale2[:, 0, :])
 
         grouped = {}
         hgrouped = {}
@@ -122,6 +133,13 @@ def tile_loralinearexpertswrapper_pb_kernel(tc, h, low_d, W_d_bytes, W_d_scale, 
             t = work.tile([P, nj * D], BF16, name="wbf", tag="wbf", bufs=4, align_bytes=64)
             nc.vector.tensor_tensor(out=t[:], in0=scale2[:, 0:nj, :].rearrange("p c k -> p (c k)"),
                                     in1=wbytes[(u, j0, nj)].bitcast(FP8), op=MULT)
+            wbf[(u, j0)] = t
+
+        def product_halves(u, j0):
+            t = work.tile([P, D], BF16, name="wbf", tag="wbf", bufs=4, align_bytes=64)
+            for g in range(PASSES):
+                ks = slice(512 * g, 512 * (g + 1))
+                nc.vector.tensor_tensor(out=t[:, ks], in0=scale2[:, 0, ks], in1=wbytes[(u, j0, 1)][:, ks].bitcast(FP8), op=MULT)
             wbf[(u, j0)] = t
 
         def turn_w(u, j0, nj):
@@ -255,9 +273,10 @@ def tile_loralinearexpertswrapper_pb_kernel(tc, h, low_d, W_d_bytes, W_d_scale, 
 
         LAST = UNITS - 1
         plain_warm(4)
+        spread_scales()
         turn_h(0, 0)
         turn_h(0, 1)
-        product(0, 0, 1)
+        product_halves(0, 0)
         product(0, 1, 1)
         plain_warm(2)
         turn_w(0, 0, 1)

@@ -86,10 +86,12 @@ def tile_loralinearexpertswrapper_pb_kernel(tc, h, low_d, W_d_bytes, W_d_scale, 
         low_sb = keep.tile([P, E * M_TILES, R], BF16, name="low_sb")
         nc.sync.dma_start(out=low_sb[:], in_=low_d.rearrange("e (m p) r -> p (e m) r", p=P))
         load_b(0)
+        load_b(E - 1)
         for e in range(1, E):
             load_w(2 * e, 0, 4)
             load_h(e)
-            load_b(e)
+            if e < E - 1:
+                load_b(e)
             load_w(2 * e + 1, 0, 4)
 
         def spread_scales():
@@ -166,7 +168,7 @@ def tile_loralinearexpertswrapper_pb_kernel(tc, h, low_d, W_d_bytes, W_d_scale, 
             tl = ps_t.tile([P, E * M_TILES, P], BF16, name="tl", tag="tp")
             for i in range(E * M_TILES):
                 nc.tensor.transpose(tl[:, i, :], low_sb[:, i, :], ident_b[:])
-            nc.scalar.activation(out=low_t[:], in_=tl[:].rearrange("p i r -> p (i r)"), func=COPY, scale=LORA_SCALE)
+            nc.scalar.copy(out=low_t[:], in_=tl[:].rearrange("p i r -> p (i r)"))
 
         def turn_b(e, half):
             if half == 0:
@@ -203,7 +205,7 @@ def tile_loralinearexpertswrapper_pb_kernel(tc, h, low_d, W_d_bytes, W_d_scale, 
                                             rhs=hq[e][:, hc].bitcast(FP8X4), rhs_scale=hs[e][:, hc],
                                             start=(g == 0), stop=(g == PASSES - 1))
                 sb = work.tile([P, 2, T], F32, name="base_t", tag="base_t", bufs=4)
-                nc.scalar.copy(out=sb[:], in_=bt[:])
+                nc.scalar.activation(out=sb[:], in_=bt[:], func=COPY, scale=1.0 / LORA_SCALE)
                 base_t[(u, half)] = sb
 
         def add_base(u):
@@ -218,23 +220,19 @@ def tile_loralinearexpertswrapper_pb_kernel(tc, h, low_d, W_d_bytes, W_d_scale, 
             r0 = (e * M_TILES + m) * P
             nc.sync.dma_start(out=out[r0:r0 + P, nh * UNIT_N:(nh + 1) * UNIT_N], in_=o[:])
 
-        def finish(u, m, on_vector):
+        def finish(u, m):
             o = work.tile([P, UNIT_N], F32, name="o_sb", tag="o_sb", bufs=4)
-            if on_vector:
-                nc.vector.tensor_copy(out=o[:], in_=fin[(u, m)][:])
-            else:
-                nc.scalar.copy(out=o[:], in_=fin[(u, m)][:])
+            nc.scalar.activation(out=o[:], in_=fin[(u, m)][:], func=COPY, scale=LORA_SCALE)
             store(u, m, o)
 
-        def lora_closed(u):
+        def lora_closed(u, m):
             e, nh = u // 2, u % 2
-            for m in range(M_TILES):
-                dl = ps_t.tile([P, UNIT_N], F32, name="dl", tag="tp")
-                nc.tensor.matmul(out=dl[:], lhsT=low_t[:, (e * M_TILES + m) * P:(e * M_TILES + m + 1) * P],
-                                 rhs=b_t[e][:, nh * UNIT_N:(nh + 1) * UNIT_N], start=True, stop=True)
-                d2 = work.tile([P, UNIT_N], F32, name="d2", tag="d2", bufs=4)
-                nc.scalar.copy(out=d2[:], in_=dl[:])
-                delta2[(u, m)] = d2
+            dl = ps_t.tile([P, UNIT_N], F32, name="dl", tag="tp")
+            nc.tensor.matmul(out=dl[:], lhsT=low_t[:, (e * M_TILES + m) * P:(e * M_TILES + m + 1) * P],
+                             rhs=b_t[e][:, nh * UNIT_N:(nh + 1) * UNIT_N], start=True, stop=True)
+            d2 = work.tile([P, UNIT_N], F32, name="d2", tag="d2", bufs=4)
+            nc.scalar.activation(out=d2[:], in_=dl[:], func=COPY, scale=LORA_SCALE)
+            delta2[(u, m)] = d2
 
         def base(u, pool, tag):
             e = u // 2
@@ -248,13 +246,47 @@ def tile_loralinearexpertswrapper_pb_kernel(tc, h, low_d, W_d_bytes, W_d_scale, 
                                         start=(g == 0), stop=(g == PASSES - 1))
                 acc[(u, m)] = a
 
-        def vadd(u):
-            for m in range(M_TILES):
-                o = work.tile([P, UNIT_N], F32, name="o_sb", tag="o_sb", bufs=4)
-                nc.vector.tensor_tensor(out=o[:], in0=acc[(u, m)][:], in1=delta2[(u, m)][:], op=ADD)
-                store(u, m, o)
+        def vadd(u, m):
+            o = work.tile([P, UNIT_N], F32, name="o_sb", tag="o_sb", bufs=4)
+            nc.vector.tensor_tensor(out=o[:], in0=acc[(u, m)][:], in1=delta2[(u, m)][:], op=ADD)
+            store(u, m, o)
 
-        PE_ADD_UNITS = UNITS - 2
+        HALF_N = UNIT_N // 2
+        half_grouped = {}
+        half_q = {}
+        half_s = {}
+
+        def turn_half(u, half):
+            half_grouped[half] = work.tile([P, PASSES, HALF_N, 4], BF16, name="half_grouped", tag="half_grouped", bufs=2, align_bytes=64)
+            for j in range(2):
+                turn_words(wbf[(u, 2 * half)][:, j * D:(j + 1) * D],
+                           half_grouped[half][:].bitcast(F32)[:, :, j * P:(j + 1) * P, :])
+
+        def quant_half(half):
+            half_q[half] = work.tile([P, PASSES * HALF_N], U32, name="half_q", tag="half_q", bufs=2, align_bytes=64)
+            half_s[half] = work.tile([P, PASSES * HALF_N], U8, name="half_s", tag="half_s", bufs=2, align_bytes=64)
+            nc.vector.quantize_mx(out=half_q[half][:].bitcast(FP8X4), scales=half_s[half][:],
+                                  in_=half_grouped[half][:].rearrange("p g n t -> p (g n t)"))
+
+        def base_half(u, half, pool, tag):
+            e = u // 2
+            for m in range(M_TILES):
+                a = pool.tile([P, HALF_N], F32, name="acc_half", tag=tag)
+                for g in range(PASSES):
+                    hc = slice(g * T + m * P, g * T + (m + 1) * P)
+                    wc = slice(g * HALF_N, (g + 1) * HALF_N)
+                    nc.tensor.matmul_mx(out=a[:], lhsT=hq[e][:, hc].bitcast(FP8X4), lhsT_scale=hs[e][:, hc],
+                                        rhs=half_q[half][:, wc].bitcast(FP8X4), rhs_scale=half_s[half][:, wc],
+                                        start=(g == 0), stop=(g == PASSES - 1))
+                acc[(u, m, half)] = a
+
+        def vadd_half(u, m, half):
+            e, nh = u // 2, u % 2
+            r0, c0 = (e * M_TILES + m) * P, nh * UNIT_N + half * HALF_N
+            o = work.tile([P, HALF_N], F32, name="o_half", tag="o_half", bufs=4)
+            nc.vector.tensor_tensor(out=o[:], in0=acc[(u, m, half)][:],
+                                    in1=delta2[(u, m)][:, half * HALF_N:(half + 1) * HALF_N], op=ADD)
+            nc.sync.dma_start(out=out[r0:r0 + P, c0:c0 + HALF_N], in_=o[:])
 
         zeros = keep.tile([P, 512], BF16, name="zeros")
         nc.vector.memset(zeros[:], 0.0)
@@ -272,8 +304,9 @@ def tile_loralinearexpertswrapper_pb_kernel(tc, h, low_d, W_d_bytes, W_d_scale, 
                                     start=True, stop=True)
 
         LAST = UNITS - 1
-        plain_warm(4)
+        plain_warm(2)
         spread_scales()
+        plain_warm(2)
         turn_h(0, 0)
         turn_h(0, 1)
         product_halves(0, 0)
@@ -285,51 +318,51 @@ def tile_loralinearexpertswrapper_pb_kernel(tc, h, low_d, W_d_bytes, W_d_scale, 
         turn_low()
         product(0, 2, 2)
         quant_h(0)
-        for s in range(UNITS):
+        for s in range(LAST):
             c = s - 1
-            more = s < LAST
-            pe_add = 0 <= c < PE_ADD_UNITS
-            if more:
-                product(s + 1, 0, 2)
-            if pe_add:
+            product(s + 1, 0, 2)
+            if c >= 0:
                 base_turned(c)
-            elif c >= 0:
-                base(c, ps_b, "bt")
             else:
                 keep_warm(4)
-            if more:
-                turn_w(s, 2, 2)
+            turn_w(s, 2, 2)
             if s == 0:
-                turn_b(0, 0)
-                turn_b(0, 1)
-            elif s % 2 == 1 and s // 2 + 1 < E:
-                turn_b(s // 2 + 1, 0)
-            elif s % 2 == 0 and s // 2 < E and s >= 2:
-                turn_b(s // 2, 1)
-            if pe_add:
+                for e in (0, E - 1):
+                    turn_b(e, 0)
+                    turn_b(e, 1)
+            elif s <= 2 * (E - 2):
+                turn_b((s + 1) // 2, (s + 1) % 2)
+            if c >= 0:
                 open_fin(c)
                 add_base(c)
-            elif more:
+            else:
                 keep_warm(2)
-            if s % 2 == 0 and s // 2 + 1 < E:
-                turn_h(s // 2 + 1, 0)
-            elif s % 2 == 1 and s // 2 + 1 < E:
-                turn_h(s // 2 + 1, 1)
-            if pe_add:
-                finish(c, 0, False)
-                finish(c, 1, False)
-            if more:
-                keep_warm(2)
-            if more:
-                product(s + 1, 2, 2)
+            if s // 2 + 1 < E:
+                turn_h(s // 2 + 1, s % 2)
+            if c >= 0:
+                finish(c, 0)
+                finish(c, 1)
+            keep_warm(2)
+            product(s + 1, 2, 2)
+            if s + 1 < LAST:
                 turn_w(s + 1, 0, 2)
-            if s + 1 == LAST:
-                turn_w(LAST, 2, 2)
-                lora_closed(LAST - 1)
-                lora_closed(LAST)
+            else:
+                turn_half(LAST, 0)
+                lora_closed(LAST - 1, 0)
+                turn_half(LAST, 1)
+                lora_closed(LAST - 1, 1)
+                lora_closed(LAST, 0)
+                lora_closed(LAST, 1)
             if s % 2 == 0 and s >= 2:
                 quant_h(s // 2)
             quant_w(s)
-        vadd(LAST - 1)
-        base(LAST, ps_f, "fin")
-        vadd(LAST)
+        base(LAST - 1, ps_b, "bt")
+        quant_half(0)
+        base_half(LAST, 0, ps_f, "fin")
+        quant_half(1)
+        base_half(LAST, 1, ps_t, "tp")
+        vadd(LAST - 1, 0)
+        vadd(LAST - 1, 1)
+        for half in range(2):
+            for m in range(M_TILES):
+                vadd_half(LAST, m, half)

@@ -314,18 +314,18 @@ def tile_loralinearexpertswrapper_pb_kernel(tc, h, low_d, W_d_bytes, W_d_scale, 
         plain_warm(2)
         turn_w(0, 0, 1)
         turn_w(0, 1, 1)
-        plain_warm(2)
-        turn_low()
         product(0, 2, 2)
+        plain_warm(2)
+        turn_w(0, 2, 2)
         quant_h(0)
         for s in range(LAST):
             c = s - 1
             product(s + 1, 0, 2)
             if c >= 0:
                 base_turned(c)
+                turn_w(c + 1, 2, 2)
             else:
-                keep_warm(4)
-            turn_w(s, 2, 2)
+                turn_low()
             if s == 0:
                 for e in (0, E - 1):
                     turn_b(e, 0)

@@ -82,9 +82,9 @@ def tile_loralinearexpertswrapper_pb_kernel(tc, h, low_d, W_d_bytes, W_d_scale, 
         load_h(0)
         load_w(0, 1, 1)
         load_w(0, 2, 2)
-        load_w(1, 0, 4)
         low_sb = keep.tile([P, E * M_TILES, R], BF16, name="low_sb")
         nc.sync.dma_start(out=low_sb[:], in_=low_d.rearrange("e (m p) r -> p (e m) r", p=P))
+        load_w(1, 0, 4)
         load_b(0)
         load_b(E - 1)
         for e in range(1, E):
@@ -314,18 +314,19 @@ def tile_loralinearexpertswrapper_pb_kernel(tc, h, low_d, W_d_bytes, W_d_scale, 
         plain_warm(2)
         turn_w(0, 0, 1)
         turn_w(0, 1, 1)
-        product(0, 2, 2)
+        product(0, 2, 1)
+        product(0, 3, 1)
         plain_warm(2)
-        turn_w(0, 2, 2)
+        turn_w(0, 2, 1)
+        turn_low()
+        turn_w(0, 3, 1)
         quant_h(0)
         for s in range(LAST):
             c = s - 1
             product(s + 1, 0, 2)
             if c >= 0:
                 base_turned(c)
-                turn_w(c + 1, 2, 2)
-            else:
-                turn_low()
+                turn_w(s, 2, 2)
             if s == 0:
                 for e in (0, E - 1):
                     turn_b(e, 0)

@@ -230,9 +230,9 @@ def tile_loralinearexpertswrapper_pb_kernel(tc, h, low_d, W_d_bytes, W_d_scale, 
             dl = ps_t.tile([P, UNIT_N], F32, name="dl", tag="tp")
             nc.tensor.matmul(out=dl[:], lhsT=low_t[:, (e * M_TILES + m) * P:(e * M_TILES + m + 1) * P],
                              rhs=b_t[e][:, nh * UNIT_N:(nh + 1) * UNIT_N], start=True, stop=True)
-            d2 = work.tile([P, UNIT_N], F32, name="d2", tag="d2", bufs=4)
-            nc.scalar.activation(out=d2[:], in_=dl[:], func=COPY, scale=LORA_SCALE)
-            delta2[(u, m)] = d2
+            if m == 0:
+                delta2[u] = work.tile([P, M_TILES, UNIT_N], F32, name="d2", tag="d2", bufs=2)
+            nc.scalar.activation(out=delta2[u][:, m, :], in_=dl[:], func=COPY, scale=LORA_SCALE)
 
         def base(u, pool, tag):
             e = u // 2
@@ -248,7 +248,7 @@ def tile_loralinearexpertswrapper_pb_kernel(tc, h, low_d, W_d_bytes, W_d_scale, 
 
         def vadd(u, m):
             o = work.tile([P, UNIT_N], F32, name="o_sb", tag="o_sb", bufs=4)
-            nc.vector.tensor_tensor(out=o[:], in0=acc[(u, m)][:], in1=delta2[(u, m)][:], op=ADD)
+            nc.vector.tensor_tensor(out=o[:], in0=acc[(u, m)][:], in1=delta2[u][:, m, :], op=ADD)
             store(u, m, o)
 
         HALF_N = UNIT_N // 2
@@ -270,23 +270,23 @@ def tile_loralinearexpertswrapper_pb_kernel(tc, h, low_d, W_d_bytes, W_d_scale, 
 
         def base_half(u, half, pool, tag):
             e = u // 2
+            a = pool.tile([P, M_TILES, HALF_N], F32, name="acc_half", tag=tag)
             for m in range(M_TILES):
-                a = pool.tile([P, HALF_N], F32, name="acc_half", tag=tag)
                 for g in range(PASSES):
                     hc = slice(g * T + m * P, g * T + (m + 1) * P)
                     wc = slice(g * HALF_N, (g + 1) * HALF_N)
-                    nc.tensor.matmul_mx(out=a[:], lhsT=hq[e][:, hc].bitcast(FP8X4), lhsT_scale=hs[e][:, hc],
+                    nc.tensor.matmul_mx(out=a[:, m, :], lhsT=hq[e][:, hc].bitcast(FP8X4), lhsT_scale=hs[e][:, hc],
                                         rhs=half_q[half][:, wc].bitcast(FP8X4), rhs_scale=half_s[half][:, wc],
                                         start=(g == 0), stop=(g == PASSES - 1))
-                acc[(u, m, half)] = a
+            acc[(u, half)] = a
 
-        def vadd_half(u, m, half):
+        def vadd_half(u, half):
             e, nh = u // 2, u % 2
-            r0, c0 = (e * M_TILES + m) * P, nh * UNIT_N + half * HALF_N
-            o = work.tile([P, HALF_N], F32, name="o_half", tag="o_half", bufs=4)
-            nc.vector.tensor_tensor(out=o[:], in0=acc[(u, m, half)][:],
-                                    in1=delta2[(u, m)][:, half * HALF_N:(half + 1) * HALF_N], op=ADD)
-            nc.sync.dma_start(out=out[r0:r0 + P, c0:c0 + HALF_N], in_=o[:])
+            c0 = nh * UNIT_N + half * HALF_N
+            o = work.tile([P, M_TILES, HALF_N], F32, name="o_half", tag="o_half", bufs=2)
+            nc.vector.tensor_tensor(out=o[:], in0=acc[(u, half)][:],
+                                    in1=delta2[u][:, :, half * HALF_N:(half + 1) * HALF_N], op=ADD)
+            nc.sync.dma_start(out=out[e * T:(e + 1) * T, c0:c0 + HALF_N].rearrange("(m p) n -> p m n", p=P), in_=o[:])
 
         zeros = keep.tile([P, 512], BF16, name="zeros")
         nc.vector.memset(zeros[:], 0.0)
@@ -340,30 +340,31 @@ def tile_loralinearexpertswrapper_pb_kernel(tc, h, low_d, W_d_bytes, W_d_scale, 
                 keep_warm(2)
             if s // 2 + 1 < E:
                 turn_h(s // 2 + 1, s % 2)
-            if c >= 0:
-                finish(c, 0)
-                finish(c, 1)
-            keep_warm(2)
-            product(s + 1, 2, 2)
             if s + 1 < LAST:
+                if c >= 0:
+                    finish(c, 0)
+                    finish(c, 1)
+                keep_warm(2)
+                product(s + 1, 2, 2)
                 turn_w(s + 1, 0, 2)
             else:
                 turn_half(LAST, 0)
-                lora_closed(LAST - 1, 0)
+                product(LAST, 2, 2)
                 turn_half(LAST, 1)
-                lora_closed(LAST - 1, 1)
-                lora_closed(LAST, 0)
-                lora_closed(LAST, 1)
+                for u in (LAST - 1, LAST):
+                    for m in range(M_TILES):
+                        lora_closed(u, m)
+                finish(c, 0)
+                finish(c, 1)
             if s % 2 == 0 and s >= 2:
                 quant_h(s // 2)
             quant_w(s)
         base(LAST - 1, ps_b, "bt")
         quant_half(0)
-        base_half(LAST, 0, ps_f, "fin")
+        base_half(LAST, 0, ps_t, "tp")
         quant_half(1)
         base_half(LAST, 1, ps_t, "tp")
         vadd(LAST - 1, 0)
         vadd(LAST - 1, 1)
         for half in range(2):
-            for m in range(M_TILES):
-                vadd_half(LAST, m, half)
+            vadd_half(LAST, half)

@@ -286,7 +286,9 @@ def tile_loralinearexpertswrapper_pb_kernel(tc, h, low_d, W_d_bytes, W_d_scale, 
             o = work.tile([P, M_TILES, HALF_N], F32, name="o_half", tag="o_half", bufs=2)
             nc.vector.tensor_tensor(out=o[:], in0=acc[(u, half)][:],
                                     in1=delta2[u][:, :, half * HALF_N:(half + 1) * HALF_N], op=ADD)
-            nc.sync.dma_start(out=out[e * T:(e + 1) * T, c0:c0 + HALF_N].rearrange("(m p) n -> p m n", p=P), in_=o[:])
+            for m in range(M_TILES):
+                r0 = (e * M_TILES + m) * P
+                nc.sync.dma_start(out=out[r0:r0 + P, c0:c0 + HALF_N], in_=o[:, m, :])
 
         zeros = keep.tile([P, 512], BF16, name="zeros")
         nc.vector.memset(zeros[:], 0.0)
@@ -335,6 +337,8 @@ def tile_loralinearexpertswrapper_pb_kernel(tc, h, low_d, W_d_bytes, W_d_scale, 
                 turn_b((s + 1) // 2, (s + 1) % 2)
             if c >= 0:
                 open_fin(c)
+                if s + 1 == LAST:
+                    turn_half(LAST, 0)
                 add_base(c)
             else:
                 keep_warm(2)
@@ -347,15 +351,16 @@ def tile_loralinearexpertswrapper_pb_kernel(tc, h, low_d, W_d_bytes, W_d_scale, 
                 keep_warm(2)
                 product(s + 1, 2, 2)
                 turn_w(s + 1, 0, 2)
+                if s == 0:
+                    lora_closed(LAST, 0)
+                    lora_closed(LAST, 1)
             else:
-                turn_half(LAST, 0)
-                product(LAST, 2, 2)
-                turn_half(LAST, 1)
-                for u in (LAST - 1, LAST):
-                    for m in range(M_TILES):
-                        lora_closed(u, m)
                 finish(c, 0)
                 finish(c, 1)
+                product(LAST, 2, 2)
+                turn_half(LAST, 1)
+                lora_closed(LAST - 1, 0)
+                lora_closed(LAST - 1, 1)
             if s % 2 == 0 and s >= 2:
                 quant_h(s // 2)
             quant_w(s)

@@ -79,17 +79,19 @@ def tile_loralinearexpertswrapper_pb_kernel(tc, h, low_d, W_d_bytes, W_d_scale, 
             b_sb[e] = t
 
         load_w(0, 0, 1)
-        load_h(0)
         load_w(0, 1, 1)
+        load_h(0)
         load_w(0, 2, 2)
         low_sb = keep.tile([P, E * M_TILES, R], BF16, name="low_sb")
         nc.sync.dma_start(out=low_sb[:], in_=low_d.rearrange("e (m p) r -> p (e m) r", p=P))
         load_w(1, 0, 4)
         load_b(0)
+        load_h(1)
         load_b(E - 1)
         for e in range(1, E):
             load_w(2 * e, 0, 4)
-            load_h(e)
+            if e > 1:
+                load_h(e)
             if e < E - 1:
                 load_b(e)
             load_w(2 * e + 1, 0, 4)
@@ -330,9 +332,8 @@ def tile_loralinearexpertswrapper_pb_kernel(tc, h, low_d, W_d_bytes, W_d_scale, 
                 base_turned(c)
                 turn_w(s, 2, 2)
             if s == 0:
-                for e in (0, E - 1):
-                    turn_b(e, 0)
-                    turn_b(e, 1)
+                turn_b(0, 0)
+                turn_b(0, 1)
             elif s <= 2 * (E - 2):
                 turn_b((s + 1) // 2, (s + 1) % 2)
             if c >= 0:
@@ -344,6 +345,9 @@ def tile_loralinearexpertswrapper_pb_kernel(tc, h, low_d, W_d_bytes, W_d_scale, 
                 keep_warm(2)
             if s // 2 + 1 < E:
                 turn_h(s // 2 + 1, s % 2)
+            if s == 0:
+                turn_b(E - 1, 0)
+                turn_b(E - 1, 1)
             if s + 1 < LAST:
                 if c >= 0:
                     finish(c, 0)

@@ -227,14 +227,19 @@ def tile_loralinearexpertswrapper_pb_kernel(tc, h, low_d, W_d_bytes, W_d_scale, 
             nc.scalar.activation(out=o[:], in_=fin[(u, m)][:], func=COPY, scale=LORA_SCALE)
             store(u, m, o)
 
+        closed = {}
+
         def lora_closed(u, m):
             e, nh = u // 2, u % 2
             dl = ps_t.tile([P, UNIT_N], F32, name="dl", tag="tp")
             nc.tensor.matmul(out=dl[:], lhsT=low_t[:, (e * M_TILES + m) * P:(e * M_TILES + m + 1) * P],
                              rhs=b_t[e][:, nh * UNIT_N:(nh + 1) * UNIT_N], start=True, stop=True)
+            closed[(u, m)] = dl
+
+        def lora_out(u, m):
             if m == 0:
                 delta2[u] = work.tile([P, M_TILES, UNIT_N], F32, name="d2", tag="d2", bufs=2)
-            nc.scalar.activation(out=delta2[u][:, m, :], in_=dl[:], func=COPY, scale=LORA_SCALE)
+            nc.scalar.activation(out=delta2[u][:, m, :], in_=closed[(u, m)][:], func=COPY, scale=LORA_SCALE)
 
         def base(u, pool, tag):
             e = u // 2
@@ -356,15 +361,19 @@ def tile_loralinearexpertswrapper_pb_kernel(tc, h, low_d, W_d_bytes, W_d_scale, 
                 product(s + 1, 2, 2)
                 turn_w(s + 1, 0, 2)
                 if s == 0:
-                    lora_closed(LAST, 0)
-                    lora_closed(LAST, 1)
+                    for m in range(M_TILES):
+                        lora_closed(LAST, m)
+                        lora_out(LAST, m)
             else:
+                for m in range(M_TILES):
+                    lora_closed(LAST - 1, m)
                 finish(c, 0)
                 finish(c, 1)
                 product(LAST, 2, 2)
                 turn_half(LAST, 1)
-                lora_closed(LAST - 1, 0)
-                lora_closed(LAST - 1, 1)
+                for m in range(M_TILES):
+                    lora_out(LAST - 1, m)
+                keep_warm(2)
             if s % 2 == 0 and s >= 2:
                 quant_h(s // 2)
             quant_w(s)

@@ -44,6 +44,9 @@ def tile_loralinearexpertswrapper_pb_kernel(tc, h, low_d, W_d_bytes, W_d_scale, 
         nc.vector.memset(warm_in[:], 0.0)
         nc.scalar.activation(out=warm_out[:], in_=warm_in[:], func=COPY)
 
+        zeros = keep.tile([P, 512], BF16, name="zeros")
+        nc.vector.memset(zeros[:].bitcast(U32), 0)
+
         ident_f = keep.tile([P, P], F32, name="ident_f")
         make_identity(nc, ident_f[:])
         ident_b = keep.tile([P, P], BF16, name="ident_b")
@@ -297,13 +300,10 @@ def tile_loralinearexpertswrapper_pb_kernel(tc, h, low_d, W_d_bytes, W_d_scale, 
                 r0 = (e * M_TILES + m) * P
                 nc.sync.dma_start(out=out[r0:r0 + P, c0:c0 + HALF_N], in_=o[:, m, :])
 
-        zeros = keep.tile([P, 512], BF16, name="zeros")
-        nc.vector.memset(zeros[:], 0.0)
-
         def plain_warm(n):
             w = ps_b.tile([P, 512], F32, name="warm_p", tag="bt")
             for i in range(n):
-                nc.tensor.matmul(out=w[:], lhsT=ident_b[:], rhs=zeros[:], start=True, stop=True)
+                nc.tensor.matmul(out=w[:], lhsT=zeros[:, 0:P], rhs=zeros[:], start=True, stop=True)
 
         def keep_warm(n):
             w = ps_b.tile([P, 512], F32, name="warm_ps", tag="bt")

from contextlib import ExitStack

import concourse.mybir as mybir
from concourse.masks import make_identity

E, T, H, D, R = 4, 256, 1024, 1024, 128
LORA_SCALE = 2.0
FLOPS = 2 * E * T * H * (D + R)

F32 = mybir.dt.float32
BF16 = mybir.dt.bfloat16
U32 = mybir.dt.uint32
U8 = mybir.dt.uint8
FP8 = mybir.dt.float8_e4m3fn
FP8X4 = mybir.dt.float8_e4m3fn_x4
MULT = mybir.AluOpType.mult
ADD = mybir.AluOpType.add
COPY = mybir.ActivationFunctionType.Copy

P = 128
PASSES = D // 512
UNIT_N = 512
UNIT_ROWTILES = UNIT_N // P
UNITS = E * H // UNIT_N
M_TILES = T // P


def tile_loralinearexpertswrapper_pb_kernel(tc, h, low_d, W_d_bytes, W_d_scale, B_d, out):
    nc = tc.nc
    with ExitStack() as ctx:
        keep = ctx.enter_context(tc.tile_pool(name="keep", bufs=1))
        work = ctx.enter_context(tc.tile_pool(name="work", bufs=3))
        ps_t = ctx.enter_context(tc.psum_pool(name="ps_t", bufs=4))
        ps_b = ctx.enter_context(tc.psum_pool(name="ps_b", bufs=2))
        ps_f = ctx.enter_context(tc.psum_pool(name="ps_f", bufs=2))
        ctx.enter_context(tc.manual_schedule())

        scale2 = keep.tile([P, 2, D], F32, name="scale2")
        scale_k = keep.tile([P, PASSES, 4], F32, name="scale_k")
        nc.sync.dma_start(out=scale_k[:], in_=W_d_scale.rearrange("a b (g p t) -> p (a b g) t", p=P, t=4))

        warm_in = keep.tile([P, 1], F32, name="warm_in")
        warm_out = keep.tile([P, 1], F32, name="warm_out")
        nc.vector.memset(warm_in[:], 0.0)
        nc.scalar.activation(out=warm_out[:], in_=warm_in[:], func=COPY)

        zeros = keep.tile([P, 512], BF16, name="zeros")
        nc.vector.memset(zeros[:].bitcast(U32), 0)

        ident_f = keep.tile([P, P], F32, name="ident_f")
        make_identity(nc, ident_f[:])
        ident_b = keep.tile([P, P], BF16, name="ident_b")
        make_identity(nc, ident_b[:])

        w_rows = W_d_bytes.rearrange("e (c p) k -> e c p k", p=P)
        h_rows = h.rearrange("e (m p) k -> e p m k", p=P)
        b_rows = B_d.rearrange("e (c p) r -> e p c r", p=P)

        wbytes = {}

        def load_w(u, j0, nj):
            e, c0 = u // 2, (u % 2) * UNIT_ROWTILES + j0
            t = keep.tile([P, nj, D], U8, name="wbytes_%d_%d" % (u, j0))
            nc.sync.dma_start(out=t[:], in_=w_rows[e, c0:c0 + nj].rearrange("c p k -> p c k"))
            for j in range(nj):
                wbytes[(u, j0 + j, 1)] = t[:, j, :]
            for j in range(0, nj - 1, 2):
                wbytes[(u, j0 + j, 2)] = t[:, j:j + 2, :].rearrange("p c k -> p (c k)")

        h_sb = {}

        def load_h(e):
            t = keep.tile([P, M_TILES, D], BF16, name="h_sb%d" % e)
            nc.sync.dma_start(out=t[:], in_=h_rows[e])
            h_sb[e] = t

        b_sb = {}

        def load_b(e):
            t = keep.tile([P, H // P, R], BF16, name="b_sb%d" % e)
            nc.sync.dma_start(out=t[:], in_=b_rows[e])
            b_sb[e] = t

        load_w(0, 0, 1)
        load_w(0, 1, 1)
        load_h(0)
        load_w(0, 2, 2)
        low_sb = keep.tile([P, E * M_TILES, R], BF16, name="low_sb")
        nc.sync.dma_start(out=low_sb[:], in_=low_d.rearrange("e (m p) r -> p (e m) r", p=P))
        load_w(1, 0, 4)
        load_b(0)
        load_h(1)
        load_b(E - 1)
        for e in range(1, E):
            load_w(2 * e, 0, 4)
            if e > 1:
                load_h(e)
            if e < E - 1:
                load_b(e)
            load_w(2 * e + 1, 0, 4)

        def spread_scales():
            for g in range(PASSES):
                sp = ps_t.tile([P, 4, P], F32, name="sp", tag="tp")
                for t in range(4):
                    nc.tensor.transpose(sp[:, t, :], scale_k[:, g, t:t + 1].to_broadcast([P, P]), ident_f[:])
                dst = scale2[:, 0, 512 * g:512 * (g + 1)].rearrange("p (n t) -> p n t", t=4)
                if g == 0:
                    nc.vector.tensor_copy(out=dst, in_=sp[:].rearrange("p t n -> p n t"))
                else:
                    nc.scalar.copy(out=dst, in_=sp[:].rearrange("p t n -> p n t"))
            nc.scalar.copy(out=scale2[:, 1, :], in_=scale2[:, 0, :])

        grouped = {}
        hgrouped = {}
        hq = {}
        hs = {}
        wq = {}
        ws = {}
        b_t = {}
        delta2 = {}
        acc = {}
        base_t = {}
        fin = {}

        def new_grouped(u):
            grouped[u] = work.tile([P, PASSES, UNIT_N, 4], BF16, name="grouped", tag="grouped", bufs=4, align_bytes=64)

        def turn_words(src_bf16, dst_words):
            words = src_bf16.bitcast(F32)
            tp = ps_t.tile([P, PASSES, 2, P], F32, name="tp", tag="tp")
            for g in range(PASSES):
                for u in range(2):
                    nc.tensor.transpose(tp[:, g, u, :], words[:, 256 * g + u:256 * (g + 1):2], ident_f[:])
            nc.scalar.copy(out=dst_words, in_=tp[:].rearrange("p g u r -> p g r u"))

        wbf = {}

        def product(u, j0, nj):
            t = work.tile([P, nj * D], BF16, name="wbf", tag="wbf", bufs=4, align_bytes=64)
            nc.vector.tensor_tensor(out=t[:], in0=scale2[:, 0:nj, :].rearrange("p c k -> p (c k)"),
                                    in1=wbytes[(u, j0, nj)].bitcast(FP8), op=MULT)
            wbf[(u, j0)] = t

        def product_halves(u, j0):
            t = work.tile([P, D], BF16, name="wbf", tag="wbf", bufs=4, align_bytes=64)
            for g in range(PASSES):
                ks = slice(512 * g, 512 * (g + 1))
                nc.vector.tensor_tensor(out=t[:, ks], in0=scale2[:, 0, ks], in1=wbytes[(u, j0, 1)][:, ks].bitcast(FP8), op=MULT)
            wbf[(u, j0)] = t

        def turn_w(u, j0, nj):
            if j0 == 0:
                new_grouped(u)
            for j in range(nj):
                turn_words(wbf[(u, j0)][:, j * D:(j + 1) * D],
                           grouped[u][:].bitcast(F32)[:, :, (j0 + j) * P:(j0 + j + 1) * P, :])

        def turn_h(e, m):
            if m == 0:
                hgrouped[e] = work.tile([P, PASSES, T, 4], BF16, name="hgrouped", tag="hgrouped", bufs=2, align_bytes=64)
            turn_words(h_sb[e][:, m, :], hgrouped[e][:].bitcast(F32)[:, :, m * P:(m + 1) * P, :])

        def quant_h(e):
            hq[e] = keep.tile([P, PASSES * T], U32, name="hq%d" % e, align_bytes=64)
            hs[e] = keep.tile([P, PASSES * T], U8, name="hs%d" % e, align_bytes=64)
            nc.vector.quantize_mx(out=hq[e][:].bitcast(FP8X4), scales=hs[e][:],
                                  in_=hgrouped[e][:].rearrange("p g n t -> p (g n t)"))

        low_t = keep.tile([P, E * T], BF16, name="low_t")

        def turn_low():
            tl = ps_t.tile([P, E * M_TILES, P], BF16, name="tl", tag="tp")
            for i in range(E * M_TILES):
                nc.tensor.transpose(tl[:, i, :], low_sb[:, i, :], ident_b[:])
            nc.scalar.copy(out=low_t[:], in_=tl[:].rearrange("p i r -> p (i r)"))

        def turn_b(e, half):
            if half == 0:
                b_t[e] = keep.tile([P, H], BF16, name="b_t%d" % e)
            tb = ps_t.tile([P, 4, P], BF16, name="tb", tag="tp")
            for c in range(4):
                nc.tensor.transpose(tb[:, c, :], b_sb[e][:, 4 * half + c, :], ident_b[:])
            nc.scalar.copy(out=b_t[e][:, 512 * half:512 * (half + 1)], in_=tb[:].rearrange("p c r -> p (c r)"))

        def open_fin(u):
            e, nh = u // 2, u % 2
            for m in range(M_TILES):
                f = ps_f.tile([P, UNIT_N], F32, name="fin", tag="fin")
                nc.tensor.matmul(out=f[:], lhsT=low_t[:, (e * M_TILES + m) * P:(e * M_TILES + m + 1) * P],
                                 rhs=b_t[e][:, nh * UNIT_N:(nh + 1) * UNIT_N], start=True, stop=False)
                fin[(u, m)] = f

        def quant_w(u):
            wq[u] = work.tile([P, PASSES * UNIT_N], U32, name="wq", tag="wq", bufs=3, align_bytes=64)
            ws[u] = work.tile([P, PASSES * UNIT_N], U8, name="ws", tag="ws", bufs=3, align_bytes=64)
            nc.vector.quantize_mx(out=wq[u][:].bitcast(FP8X4), scales=ws[u][:],
                                  in_=grouped[u][:].rearrange("p g n t -> p (g n t)"))

        def base_turned(u):
            e = u // 2
            for half in range(2):
                bt = ps_b.tile([P, 2, T], F32, name="bt", tag="bt")
                for cc in range(2):
                    c = half * 2 + cc
                    for g in range(PASSES):
                        wc = slice(g * UNIT_N + c * P, g * UNIT_N + (c + 1) * P)
                        hc = slice(g * T, (g + 1) * T)
                        nc.tensor.matmul_mx(out=bt[:, cc, :], lhsT=wq[u][:, wc].bitcast(FP8X4), lhsT_scale=ws[u][:, wc],
                                            rhs=hq[e][:, hc].bitcast(FP8X4), rhs_scale=hs[e][:, hc],
                                            start=(g == 0), stop=(g == PASSES - 1))
                sb = work.tile([P, 2, T], F32, name="base_t", tag="base_t", bufs=4)
                nc.scalar.activation(out=sb[:], in_=bt[:], func=COPY, scale=1.0 / LORA_SCALE)
                base_t[(u, half)] = sb

        def add_base(u):
            for m in range(M_TILES):
                for c in range(4):
                    nc.tensor.matmul(out=fin[(u, m)][:, c * P:(c + 1) * P],
                                     lhsT=base_t[(u, c // 2)][:, c % 2, m * P:(m + 1) * P], rhs=ident_f[:],
                                     is_transpose=True, start=False, stop=(c == 3))

        def store(u, m, o):
            e, nh = u // 2, u % 2
            r0 = (e * M_TILES + m) * P
            nc.sync.dma_start(out=out[r0:r0 + P, nh * UNIT_N:(nh + 1) * UNIT_N], in_=o[:])

        def finish(u, m):
            o = work.tile([P, UNIT_N], F32, name="o_sb", tag="o_sb", bufs=4)
            nc.scalar.activation(out=o[:], in_=fin[(u, m)][:], func=COPY, scale=LORA_SCALE)
            store(u, m, o)

        closed = {}

        def lora_closed(u, m):
            e, nh = u // 2, u % 2
            dl = ps_t.tile([P, UNIT_N], F32, name="dl", tag="tp")
            nc.tensor.matmul(out=dl[:], lhsT=low_t[:, (e * M_TILES + m) * P:(e * M_TILES + m + 1) * P],
                             rhs=b_t[e][:, nh * UNIT_N:(nh + 1) * UNIT_N], start=True, stop=True)
            closed[(u, m)] = dl

        def lora_out(u, m):
            if m == 0:
                delta2[u] = work.tile([P, M_TILES, UNIT_N], F32, name="d2", tag="d2", bufs=2)
            nc.scalar.activation(out=delta2[u][:, m, :], in_=closed[(u, m)][:], func=COPY, scale=LORA_SCALE)

        def base(u, pool, tag):
            e = u // 2
            for m in range(M_TILES):
                a = pool.tile([P, UNIT_N], F32, name="acc", tag=tag)
                for g in range(PASSES):
                    hc = slice(g * T + m * P, g * T + (m + 1) * P)
                    wc = slice(g * UNIT_N, (g + 1) * UNIT_N)
                    nc.tensor.matmul_mx(out=a[:], lhsT=hq[e][:, hc].bitcast(FP8X4), lhsT_scale=hs[e][:, hc],
                                        rhs=wq[u][:, wc].bitcast(FP8X4), rhs_scale=ws[u][:, wc],
                                        start=(g == 0), stop=(g == PASSES - 1))
                acc[(u, m)] = a

        def vadd(u, m):
            o = work.tile([P, UNIT_N], F32, name="o_sb", tag="o_sb", bufs=4)
            nc.vector.tensor_tensor(out=o[:], in0=acc[(u, m)][:], in1=delta2[u][:, m, :], op=ADD)
            store(u, m, o)

        HALF_N = UNIT_N // 2
        half_grouped = {}
        half_q = {}
        half_s = {}

        def turn_half(u, half):
            half_grouped[half] = work.tile([P, PASSES, HALF_N, 4], BF16, name="half_grouped", tag="half_grouped", bufs=2, align_bytes=64)
            for j in range(2):
                turn_words(wbf[(u, 2 * half)][:, j * D:(j + 1) * D],
                           half_grouped[half][:].bitcast(F32)[:, :, j * P:(j + 1) * P, :])

        def quant_half(half):
            half_q[half] = work.tile([P, PASSES * HALF_N], U32, name="half_q", tag="half_q", bufs=2, align_bytes=64)
            half_s[half] = work.tile([P, PASSES * HALF_N], U8, name="half_s", tag="half_s", bufs=2, align_bytes=64)
            nc.vector.quantize_mx(out=half_q[half][:].bitcast(FP8X4), scales=half_s[half][:],
                                  in_=half_grouped[half][:].rearrange("p g n t -> p (g n t)"))

        def base_half(u, half, pool, tag):
            e = u // 2
            a = pool.tile([P, M_TILES, HALF_N], F32, name="acc_half", tag=tag)
            for m in range(M_TILES):
                for g in range(PASSES):
                    hc = slice(g * T + m * P, g * T + (m + 1) * P)
                    wc = slice(g * HALF_N, (g + 1) * HALF_N)
                    nc.tensor.matmul_mx(out=a[:, m, :], lhsT=hq[e][:, hc].bitcast(FP8X4), lhsT_scale=hs[e][:, hc],
                                        rhs=half_q[half][:, wc].bitcast(FP8X4), rhs_scale=half_s[half][:, wc],
                                        start=(g == 0), stop=(g == PASSES - 1))
            acc[(u, half)] = a

        def vadd_half(u, half):
            e, nh = u // 2, u % 2
            c0 = nh * UNIT_N + half * HALF_N
            o = work.tile([P, M_TILES, HALF_N], F32, name="o_half", tag="o_half", bufs=2)
            nc.vector.tensor_tensor(out=o[:], in0=acc[(u, half)][:],
                                    in1=delta2[u][:, :, half * HALF_N:(half + 1) * HALF_N], op=ADD)
            for m in range(M_TILES):
                r0 = (e * M_TILES + m) * P
                nc.sync.dma_start(out=out[r0:r0 + P, c0:c0 + HALF_N], in_=o[:, m, :])

        def plain_warm(n):
            w = ps_b.tile([P, 512], F32, name="warm_p", tag="bt")
            for i in range(n):
                nc.tensor.matmul(out=w[:], lhsT=zeros[:, 0:P], rhs=zeros[:], start=True, stop=True)

        def keep_warm(n):
            w = ps_b.tile([P, 512], F32, name="warm_ps", tag="bt")
            for i in range(n):
                nc.tensor.matmul_mx(out=w[:], lhsT=hq[0][:, 0:P].bitcast(FP8X4), lhsT_scale=hs[0][:, 0:P],
                                    rhs=hq[0][:, 0:512].bitcast(FP8X4), rhs_scale=hs[0][:, 0:512],
                                    start=True, stop=True)

        LAST = UNITS - 1
        plain_warm(2)
        spread_scales()
        plain_warm(2)
        turn_h(0, 0)
        turn_h(0, 1)
        product_halves(0, 0)
        product(0, 1, 1)
        plain_warm(2)
        turn_w(0, 0, 1)
        turn_w(0, 1, 1)
        product(0, 2, 1)
        product(0, 3, 1)
        plain_warm(2)
        turn_w(0, 2, 1)
        turn_low()
        turn_w(0, 3, 1)
        quant_h(0)
        for s in range(LAST):
            c = s - 1
            product(s + 1, 0, 2)
            if c >= 0:
                base_turned(c)
                turn_w(s, 2, 2)
            if s == 0:
                turn_b(0, 0)
                turn_b(0, 1)
            elif s <= 2 * (E - 2):
                turn_b((s + 1) // 2, (s + 1) % 2)
            if c >= 0:
                open_fin(c)
                if s + 1 == LAST:
                    turn_half(LAST, 0)
                add_base(c)
            else:
                keep_warm(2)
            if s // 2 + 1 < E:
                turn_h(s // 2 + 1, s % 2)
            if s == 0:
                turn_b(E - 1, 0)
                turn_b(E - 1, 1)
            if s + 1 < LAST:
                if c >= 0:
                    finish(c, 0)
                    finish(c, 1)
                keep_warm(2)
                product(s + 1, 2, 2)
                turn_w(s + 1, 0, 2)
                if s == 0:
                    for m in range(M_TILES):
                        lora_closed(LAST, m)
                        lora_out(LAST, m)
            else:
                for m in range(M_TILES):
                    lora_closed(LAST - 1, m)
                finish(c, 0)
                finish(c, 1)
                product(LAST, 2, 2)
                turn_half(LAST, 1)
                for m in range(M_TILES):
                    lora_out(LAST - 1, m)
                keep_warm(2)
            if s % 2 == 0 and s >= 2:
                quant_h(s // 2)
            quant_w(s)
        base(LAST - 1, ps_b, "bt")
        quant_half(0)
        base_half(LAST, 0, ps_t, "tp")
        quant_half(1)
        base_half(LAST, 1, ps_t, "tp")
        vadd(LAST - 1, 0)
        vadd(LAST - 1, 1)
        for half in range(2):
            vadd_half(LAST, half)
